import numpy as np
import ml_dtypes


def mxq(x, axis, fmt="e4m3"):
    dtype, down = {"e4m3": (ml_dtypes.float8_e4m3fn, 7), "e5m2": (ml_dtypes.float8_e5m2, 14)}[fmt]
    v = np.moveaxis(np.asarray(x, np.float32).astype(ml_dtypes.bfloat16).astype(np.float64), axis, -1)
    blocks = v.reshape(v.shape[:-1] + (-1, 32))
    amax = np.abs(blocks).max(-1, keepdims=True)
    byte = np.maximum(np.where(amax > 0, np.frexp(amax)[1] - 1 + 127, 0) - down, 1)
    scale = np.exp2(byte - 127.0)
    codes = (blocks / scale).astype(np.float32).astype(dtype).astype(np.float64)
    return np.moveaxis((codes * scale).reshape(v.shape), -1, axis)


WIDE = False


def mx_kscale(k):
    if not WIDE:
        return np.ones(k)
    levels = np.array([30, -30])
    if k % 512:
        return np.exp2(np.random.permutation(np.resize(levels, k // 32))).repeat(32)
    a = np.empty((k // 512, 16))
    for p in range(k // 512):
        a[p, :8] = np.random.permutation(np.resize(levels, 8))
        for g in range(8):
            far = levels[np.abs(levels - a[p, g]) >= 10]
            a[p, g + 8] = far[np.random.randint(len(far))]
    return np.exp2(a.ravel()).repeat(32)


BF16 = ml_dtypes.bfloat16


def bf(x):
    return np.asarray(x, np.float32).astype(BF16)


def f64(x):
    return np.asarray(x).astype(np.float64)


T, B, I, H = 16, 128, 512, 1024


def sigmoid(v):
    return 1.0 / (1.0 + np.exp(-v))


def setup_inputs():
    s = mx_kscale(I)
    return {"input_seq": bf(np.random.standard_normal((T, B, I)) * s),
            "W_ih": bf(np.random.standard_normal((3 * H, I)) / np.sqrt(I) / s[None, :]),
            "b_ih": bf(np.random.standard_normal(3 * H) * 0.3),
            "gh": bf(np.random.standard_normal((B, 3 * H)) * 0.5)}


def reference(input_seq, W_ih, b_ih, gh):
    gi = (mxq(f64(input_seq), 2, "e5m2") @ mxq(f64(W_ih), 1, "e4m3").T) + f64(b_ih)
    g = f64(gh)
    i_r, i_z, i_n = gi[..., :H], gi[..., H:2 * H], gi[..., 2 * H:]
    h_r, h_z, h_n = g[..., :H], g[..., H:2 * H], g[..., 2 * H:]
    r = sigmoid(i_r + h_r)
    z = sigmoid(i_z + h_z)
    n = np.tanh(i_n + r * h_n)
    h = (1.0 - z) * n
    return np.transpose(h, (1, 0, 2))

@@ -1,0 +1,420 @@
+from contextlib import ExitStack
+
+import concourse.mybir as mybir
+from concourse.masks import make_identity
+
+T, B, K, H = 16, 128, 512, 1024
+FLOPS = 2 * T * B * K * 3 * H
+
+F32 = mybir.dt.float32
+BF16 = mybir.dt.bfloat16
+U32 = mybir.dt.uint32
+U8 = mybir.dt.uint8
+X_FORMAT = mybir.dt.float8_e5m2_x4
+W_FORMAT = mybir.dt.float8_e4m3fn_x4
+ADD = mybir.AluOpType.add
+MULT = mybir.AluOpType.mult
+SIGMOID = mybir.ActivationFunctionType.Sigmoid
+TANH = mybir.ActivationFunctionType.Tanh
+
+P = 128
+BANK = 512
+PACK = 4
+ROWS = 256
+TG = 4
+GROUPS = T // TG
+PAIRS = H // ROWS
+STEPS = PAIRS * GROUPS * 2
+R, Z, N = 0, 1, 2
+MX_BANKS = 4
+TR_BANKS = 2
+BACK_BANKS = 2
+W1_SLOTS = (-3, 0, -1, -2, 1, -2, 2)
+X3V = False
+X3B = 4
+WQ_SLOTS = (-6, -5, -4, -3, -2, -2, -2)
+WZN0 = 1
+X2B = 2
+V_LAST = 0
+E_LAG = 3
+Z_LAG = 3
+T_LAG = E_LAG + 1
+F_LAG = E_LAG + 2
+Q_STEPS = [s for s in range(STEPS - 2) if s % 2 == 0]
+X_SLOTS = (-3, -2, -2)
+HEAD_ENG = "svsvsvs"
+V_COPY_UNTIL = 1
+
+
+def tile_grucellmodel_pa_kernel(tc, input_seq, W_ih, b_ih, gh, out):
+    nc = tc.nc
+    x_blocks = input_seq.rearrange("t b k -> (t b) k").rearrange("(g h p j) k -> g p h (j k)", h=2, p=P, j=2)
+    w_blocks = W_ih.rearrange("(gate pair p j) k -> pair p gate (j k)", gate=3, p=P, j=2)
+    gh_gates = gh.rearrange("b (gate c) -> b gate c", gate=3)
+
+    with ExitStack() as ctx:
+        keep = ctx.enter_context(tc.tile_pool(name="keep", bufs=1))
+        work = ctx.enter_context(tc.tile_pool(name="work", bufs=4))
+        psum = ctx.enter_context(tc.psum_pool(name="psum", bufs=1))
+        ctx.enter_context(tc.manual_schedule())
+
+        def mx_bank():
+            return psum.tile([P, BANK], F32, name="mx_bank", tag="mx", bufs=MX_BANKS)
+
+        def plain_bank(tag="plain"):
+            return psum.tile([P, BANK], F32, name="plain_bank", tag=tag, bufs=2)
+
+        x_raw = {}
+        w_raw = {}
+        gh_raw = {}
+
+        def load_x(g, halves):
+            raw = keep.tile([P, len(halves), 2 * K], BF16, name="x_raw_%d_%d" % (g, halves[0]))
+            nc.sync.dma_start(out=raw[:], in_=x_blocks[g][:, halves[0] : halves[-1] + 1, :])
+            for i, h in enumerate(halves):
+                x_raw[g, h] = raw[:, i, :]
+
+        def load_w(pair, gates):
+            raw = keep.tile([P, len(gates), 2 * K], BF16, name="w_raw_%d_%d" % (pair, gates[0]))
+            nc.sync.dma_start(out=raw[:], in_=w_blocks[pair][:, gates[0] : gates[-1] + 1, :])
+            for i, gate in enumerate(gates):
+                w_raw[pair, gate] = raw[:, i, :]
+
+        def load_gh(pairs):
+            raw = keep.tile([P, 3, len(pairs) * ROWS], BF16, name="gh_raw_%d" % pairs[0])
+            nc.sync.dma_start(out=raw[:], in_=gh_gates[:, :, pairs[0] * ROWS : (pairs[-1] + 1) * ROWS])
+            for i, pair in enumerate(pairs):
+                gh_raw[pair] = raw[:, :, i * ROWS : (i + 1) * ROWS]
+
+        bias_rows = keep.tile([P, P], BF16, name="bias_rows")
+        nc.vector.memset(bias_rows[:], 0.0)
+        nc.scalar.dma_start(out=bias_rows[0 : 3 * H // P, :], in_=b_ih.rearrange("(c p) -> c p", p=P))
+
+        load_x(0, [0])
+        load_w(0, [R])
+        load_x(0, [1])
+        load_gh([0])
+        load_x(1, [0])
+        load_x(1, [1])
+        load_w(0, [N])
+        load_w(0, [Z])
+        load_x(2, [0, 1])
+        load_x(3, [0, 1])
+        load_gh([1, 2, 3])
+        load_w(1, [R, Z, N])
+        load_w(2, [R, Z, N])
+        load_w(3, [R, Z, N])
+
+        ident32 = keep.tile([P, P], F32, name="ident32")
+        make_identity(nc, ident32[:])
+        ident16 = keep.tile([P, P], BF16, name="ident16")
+        make_identity(nc, ident16[:])
+
+        x_codes = [keep.tile([P, TG * B], U32, name="x_codes_%d" % g, align_bytes=64) for g in range(GROUPS)]
+        x_scales = [keep.tile([P, TG * B], U8, name="x_scales_%d" % g, align_bytes=64) for g in range(GROUPS)]
+        w_codes = [keep.tile([P, 3 * ROWS], U32, name="w_codes_%d" % q, align_bytes=64) for q in range(PAIRS)]
+        w_scales = [keep.tile([P, 3 * ROWS], U8, name="w_scales_%d" % q, align_bytes=64) for q in range(PAIRS)]
+        x_grouped = [keep.tile([P, TG * B * PACK], BF16, name="x_grouped_%d" % g, align_bytes=64) for g in range(GROUPS)]
+        w_grouped = [keep.tile([P, 3 * ROWS * PACK], BF16, name="w_grouped_%d" % q, align_bytes=64) for q in range(PAIRS)]
+        gh_t = [keep.tile([P, 4, B], F32, name="gh_t_%d" % q) for q in range(PAIRS)]
+        c_z = [keep.tile([P, ROWS], F32, name="c_z_%d" % q) for q in range(PAIRS)]
+        bias_t = keep.tile([P, 32], F32, name="bias_t")
+        turned = {}
+
+        def copy_on(engine, dst, src):
+            if engine is nc.scalar:
+                nc.scalar.copy(out=dst, in_=src)
+            else:
+                nc.vector.tensor_copy(out=dst, in_=src)
+
+        def turn(key, raw, tag="plain"):
+            bank = plain_bank(tag)
+            words = raw.bitcast(F32)
+            for j in range(2):
+                for u in range(2):
+                    c = (2 * j + u) * P
+                    nc.tensor.transpose(bank[:, c : c + P], words[:, j * 256 + u : (j + 1) * 256 : 2], ident32[:])
+            turned[key] = bank
+
+        def interleave(key, grouped, block, engine):
+            dst = grouped[:, block * ROWS * PACK : (block + 1) * ROWS * PACK].bitcast(F32)
+            copy_on(
+                engine,
+                dst.rearrange("q (p j u) -> q p j u", j=2, u=2),
+                turned[key][:].rearrange("q (j u p) -> q p j u", j=2, u=2),
+            )
+
+        def quantize(fmt, codes, scales, grouped, first, count):
+            cols = slice(first * ROWS, (first + count) * ROWS)
+            nc.vector.quantize_mx(
+                out=codes[:, cols].bitcast(fmt),
+                scales=scales[:, cols],
+                in_=grouped[:, first * ROWS * PACK : (first + count) * ROWS * PACK],
+            )
+
+        def turn_gh(pair, tag="plain"):
+            bank = plain_bank(tag)
+            for i, gate in enumerate((R, N)):
+                for j in range(2):
+                    c = (2 * i + j) * P
+                    nc.tensor.matmul(
+                        bank[:, c : c + P], lhsT=gh_raw[pair][:, gate, j * P : (j + 1) * P], rhs=ident16[:],
+                        start=True, stop=True,
+                    )
+            turned["gh", pair] = bank
+
+        def spread_z(pair):
+            bank = plain_bank()
+            nc.tensor.matmul(bank[:, 0:ROWS], lhsT=ident16[:], rhs=gh_raw[pair][:, Z, :], start=True, stop=False)
+            for j in range(2):
+                c = H // P + 2 * pair + j
+                nc.tensor.matmul(
+                    bank[:, j * P : (j + 1) * P], lhsT=ident16[:, c : c + 1].to_broadcast([P, P]), rhs=bias_rows[:],
+                    start=False, stop=(j == 1),
+                )
+            turned["cz", pair] = bank
+
+        def turn_bias():
+            bank = mx_bank()
+            nc.tensor.matmul(bank[:, 0:32], lhsT=bias_rows[:], rhs=ident16[:, 0:32], start=True, stop=True)
+            nc.vector.tensor_copy(out=bias_t[:], in_=bank[:, 0:32])
+
+        def keep_gh(pair, engine):
+            copy_on(engine, gh_t[pair][:].rearrange("p i b -> p (i b)"), turned["gh", pair][:])
+
+        def keep_cz(pair, engine):
+            copy_on(engine, c_z[pair][:], turned["cz", pair][:, 0:ROWS])
+
+        def place(s):
+            return s // (2 * GROUPS), (s // 2) % GROUPS, s % 2
+
+        sums = {}
+        vals = {}
+
+        def multiply(s, gate):
+            pair, g, j = place(s)
+            bank = mx_bank()
+            if gate == Z:
+                w_cols = slice(Z * ROWS, (Z + 1) * ROWS)
+                for i in range(2):
+                    x_cols = slice((2 * j + i) * B, (2 * j + i + 1) * B)
+                    nc.tensor.matmul_mx(
+                        out=bank[:, i * ROWS : (i + 1) * ROWS],
+                        lhsT=x_codes[g][:, x_cols].bitcast(X_FORMAT), lhsT_scale=x_scales[g][:, x_cols],
+                        rhs=w_codes[pair][:, w_cols].bitcast(W_FORMAT), rhs_scale=w_scales[pair][:, w_cols],
+                        start=True, stop=True,
+                    )
+            else:
+                w_cols = slice(gate * ROWS + j * P, gate * ROWS + (j + 1) * P)
+                nc.tensor.matmul_mx(
+                    out=bank[:],
+                    lhsT=w_codes[pair][:, w_cols].bitcast(W_FORMAT), lhsT_scale=w_scales[pair][:, w_cols],
+                    rhs=x_codes[g][:].bitcast(X_FORMAT), rhs_scale=x_scales[g][:],
+                    start=True, stop=True,
+                )
+            sums[s, gate] = bank
+
+        def by_t(ap):
+            return ap.rearrange("p (t b) -> p t b", b=P)
+
+        def bias(s, gate):
+            pair, g, j = place(s)
+            c = gate * (H // P) + 2 * pair + j
+            return bias_t[:, c : c + 1]
+
+        def add_r(s):
+            pair, g, j = place(s)
+            pre_r = work.tile([P, BANK], F32, name="pre_r", bufs=4)
+            nc.vector.tensor_tensor(
+                out=by_t(pre_r[:]), in0=by_t(sums[s, R][:]),
+                in1=gh_t[pair][:, j : j + 1, :].to_broadcast([P, TG, B]), op=ADD,
+            )
+            vals["pre_r", s] = pre_r
+
+        def gate_r(s):
+            r = work.tile([P, BANK], F32, name="r", bufs=4)
+            nc.scalar.activation(out=r[:], in_=vals["pre_r", s][:], func=SIGMOID, bias=bias(s, R))
+            vals["r", s] = r
+
+        def scale_hn(s, engine):
+            pair, g, j = place(s)
+            rh = work.tile([P, BANK], F32, name="rh", bufs=5)
+            engine.tensor_tensor(
+                out=by_t(rh[:]), in0=by_t(vals["r", s][:]),
+                in1=gh_t[pair][:, 2 + j : 3 + j, :].to_broadcast([P, TG, B]), op=MULT,
+            )
+            vals["rh", s] = rh
+
+        def add_z(s):
+            pair, g, j = place(s)
+            pre_z = work.tile([P, 2, ROWS], F32, name="pre_z", bufs=4)
+            nc.vector.tensor_tensor(
+                out=pre_z[:], in0=sums[s, Z][:].rearrange("p (t c) -> p t c", t=2),
+                in1=c_z[pair][:].unsqueeze(1).to_broadcast([P, 2, ROWS]), op=ADD,
+            )
+            vals["pre_z", s] = pre_z
+
+        def gate_z(s):
+            j = s % 2
+            if j == 0:
+                vals["keep_z", s // 2] = work.tile([P, TG, ROWS], F32, name="not_z", bufs=4)
+            nc.scalar.activation(
+                out=vals["keep_z", s // 2][:, 2 * j : 2 * j + 2, :], in_=vals["pre_z", s][:], func=SIGMOID, scale=-1.0
+            )
+
+        def add_n(s):
+            pre_n = work.tile([P, BANK], F32, name="pre_n", bufs=4)
+            if s in Q_STEPS:
+                nc.vector.scalar_tensor_tensor(
+                    out=pre_n[:], in0=sums[s, N][:], scalar=bias(s, N), in1=vals["rh", s][:], op0=ADD, op1=ADD
+                )
+            else:
+                nc.vector.tensor_tensor(out=pre_n[:], in0=sums[s, N][:], in1=vals["rh", s][:], op=ADD)
+            vals["pre_n", s] = pre_n
+
+        def tanh_first(s):
+            n = work.tile([P, BANK], F32, name="n_first", bufs=4)
+            nc.scalar.activation(out=n[:], in_=vals["pre_n", s][:], func=TANH, bias=bias(s, N))
+            vals["n", s] = n
+
+        def turn_back(s):
+            src = vals["pre_n", s] if s in Q_STEPS else vals["n", s]
+            bank = plain_bank("back")
+            for t in range(TG):
+                nc.tensor.transpose(bank[:, t * P : (t + 1) * P], src[:, t * B : (t + 1) * B], ident32[:])
+            vals["turned", s] = bank
+
+        def tanh_last(s):
+            n = work.tile([P, BANK], F32, name="n_last", bufs=4)
+            nc.scalar.activation(out=n[:], in_=vals["turned", s][:], func=TANH)
+            vals["n", s] = n
+
+        def finish(s):
+            pair, g, j = place(s)
+            if j == 0:
+                vals["h", s // 2] = work.tile([P, TG, ROWS], F32, name="h", bufs=4)
+            h = vals["h", s // 2][:, :, j * P : (j + 1) * P]
+            not_z = vals["keep_z", s // 2][:, :, j * P : (j + 1) * P]
+            if s in Q_STEPS:
+                nc.gpsimd.tensor_tensor(out=h, in0=by_t(vals["n", s][:]), in1=not_z, op=MULT)
+            else:
+                nc.vector.tensor_tensor(out=h, in0=by_t(vals["turned", s][:]), in1=not_z, op=MULT)
+            rows = out[:, TG * g : TG * (g + 1), :]
+            if s >= STEPS - 2:
+                c = pair * ROWS + j * P
+                nc.sync.dma_start(out=rows[:, :, c : c + P], in_=h)
+            elif j == 1:
+                nc.sync.dma_start(out=rows[:, :, pair * ROWS : (pair + 1) * ROWS], in_=vals["h", s // 2][:])
+
+        turn(("x", 0, 0), x_raw[0, 0])
+        turn(("w", 0, R), w_raw[0, R])
+        turn(("x", 0, 1), x_raw[0, 1], "back")
+        turn_gh(0, "back")
+        interleave(("x", 0, 0), x_grouped[0], 0, nc.scalar)
+        interleave(("w", 0, R), w_grouped[0], R, nc.vector)
+        interleave(("x", 0, 1), x_grouped[0], 1, nc.scalar)
+        quantize(X_FORMAT, x_codes[0], x_scales[0], x_grouped[0], 0, 1)
+        quantize(W_FORMAT, w_codes[0], w_scales[0], w_grouped[0], R, 1)
+        quantize(X_FORMAT, x_codes[0], x_scales[0], x_grouped[0], 1, 1)
+        keep_gh(0, nc.scalar)
+        turn_bias()
+        turn(("x", 1, 0), x_raw[1, 0])
+        multiply(0, R)
+        multiply(1, R)
+        turn(("x", 1, 1), x_raw[1, 1])
+        interleave(("x", 1, 0), x_grouped[1], 0, nc.vector)
+        interleave(("x", 1, 1), x_grouped[1], 1, nc.scalar)
+        turn(("w", 0, N), w_raw[0, N], "back")
+        turn(("w", 0, Z), w_raw[0, Z], "back")
+
+        turns = {}
+        copies = {}
+        v_copies = {}
+        quants = {}
+        early_quants = {}
+
+        def ride(slot, turn_job, copy_job, on_vector=False):
+            turns.setdefault(slot - 1, []).append(turn_job)
+            if on_vector:
+                v_copies.setdefault(slot, []).append(lambda: copy_job(nc.vector))
+            else:
+                copies.setdefault(slot, []).append(lambda: copy_job(nc.scalar))
+
+        def ride_x(slot, g, h, v=False):
+            ride(slot, lambda: turn(("x", g, h), x_raw[g, h]), lambda e: interleave(("x", g, h), x_grouped[g], h, e), v)
+
+        def ride_w(slot, q, gate, v=False):
+            ride(slot, lambda: turn(("w", q, gate), w_raw[q, gate]), lambda e: interleave(("w", q, gate), w_grouped[q], gate, e), v)
+
+        def quant_x(slot, g, table=early_quants):
+            table.setdefault(slot, []).append(lambda: quantize(X_FORMAT, x_codes[g], x_scales[g], x_grouped[g], 0, 2))
+
+        def quant_w(slot, q, first, count, table=early_quants):
+            table.setdefault(slot, []).append(lambda: quantize(W_FORMAT, w_codes[q], w_scales[q], w_grouped[q], first, count))
+
+        quant_x(0, 1, quants)
+        v_copies[0] = [lambda: interleave(("w", 0, N), w_grouped[0], N, nc.vector)]
+        copies[1] = [lambda: interleave(("w", 0, Z), w_grouped[0], Z, nc.scalar)]
+        quant_w(WZN0, 0, Z, 2, quants)
+        ride(1, lambda: spread_z(0), lambda e: keep_cz(0, e), True)
+        ride_x(1, 2, 0)
+        ride_x(2, 2, 1)
+        quant_x(2, 2, quants)
+        ride_x(3, 3, 0, X3V)
+        ride_x(X3B, 3, 1)
+        quant_x(4, 3, early_quants if X3B == 3 else quants)
+        for q in range(1, PAIRS):
+            first = 8 * q
+            slots = W1_SLOTS if q == 1 else WQ_SLOTS
+            ride_w(first + slots[0], q, R)
+            ride_w(first + slots[1], q, Z)
+            ride_w(first + slots[2], q, N)
+            ride(first + slots[3], lambda q=q: turn_gh(q), lambda e, q=q: keep_gh(q, e))
+            ride(first + slots[4], lambda q=q: spread_z(q), lambda e, q=q: keep_cz(q, e))
+            if q == 1:
+                quant_w(first + slots[5], q, R, 1)
+                quant_w(first + slots[6], q, Z, 2)
+            else:
+                quant_w(first + slots[5], q, R, 2)
+                quant_w(first + slots[6], q, N, 1)
+
+        def live(s):
+            return 0 <= s < STEPS
+
+        for slot in range(STEPS + F_LAG):
+            for job in copies.get(slot, []):
+                job()
+            if live(slot):
+                add_r(slot)
+                gate_r(slot)
+                if slot < STEPS - V_LAST:
+                    scale_hn(slot, nc.gpsimd)
+            for job in early_quants.get(slot, []):
+                job()
+            for job in v_copies.get(slot, []):
+                job()
+            if live(slot - T_LAG):
+                turn_back(slot - T_LAG)
+            for job in turns.get(slot, []):
+                job()
+            if live(slot - 1) and slot - 1 >= STEPS - V_LAST:
+                scale_hn(slot - 1, nc.vector)
+            if live(slot - E_LAG):
+                add_n(slot - E_LAG)
+                if slot - E_LAG not in Q_STEPS:
+                    tanh_first(slot - E_LAG)
+            if live(slot - T_LAG) and slot - T_LAG in Q_STEPS:
+                tanh_last(slot - T_LAG)
+            if live(slot - Z_LAG):
+                add_z(slot - Z_LAG)
+                gate_z(slot - Z_LAG)
+            if live(slot - F_LAG):
+                finish(slot - F_LAG)
+            for job in quants.get(slot, []):
+                job()
+            if live(slot - E_LAG + 1):
+                multiply(slot - E_LAG + 1, N)
+            if live(slot - Z_LAG + 1):
+                multiply(slot - Z_LAG + 1, Z)
+            if live(slot + 2):
+                multiply(slot + 2, R)

@@ -36,6 +36,7 @@ WQ_SLOTS = (-6, -5, -4, -3, -2, -2, -2)
 WZN0 = 1
 X2B = 2
 V_LAST = 0
+WARM = (5, 1)
 E_LAG = 3
 Z_LAG = 3
 T_LAG = E_LAG + 1
@@ -89,6 +90,18 @@ def tile_grucellmodel_pa_kernel(tc, input_seq, W_ih, b_ih, gh, out):
         bias_rows = keep.tile([P, P], BF16, name="bias_rows")
         nc.vector.memset(bias_rows[:], 0.0)
         nc.scalar.dma_start(out=bias_rows[0 : 3 * H // P, :], in_=b_ih.rearrange("(c p) -> c p", p=P))
+
+        zeros = keep.tile([P, BANK], BF16, name="zeros")
+        nc.vector.memset(zeros[:], 0.0)
+        unread = keep.tile([P, 1], F32, name="unread")
+        nc.scalar.activation(out=unread[:], in_=zeros[:, 0:1], func=SIGMOID)
+
+        def warm_up(count):
+            bank = mx_bank()
+            for i in range(count):
+                nc.tensor.matmul(bank[:], lhsT=zeros[:, 0:P], rhs=zeros[:], start=True, stop=True)
+
+        warm_up(WARM[0])
 
         load_x(0, [0])
         load_w(0, [R])
@@ -309,6 +322,7 @@ def tile_grucellmodel_pa_kernel(tc, input_seq, W_ih, b_ih, gh, out):
         turn(("x", 0, 0), x_raw[0, 0])
         turn(("w", 0, R), w_raw[0, R])
         turn(("x", 0, 1), x_raw[0, 1], "back")
+        warm_up(WARM[1])
         turn_gh(0, "back")
         interleave(("x", 0, 0), x_grouped[0], 0, nc.scalar)
         interleave(("w", 0, R), w_grouped[0], R, nc.vector)

@@ -20,31 +20,27 @@ TANH = mybir.ActivationFunctionType.Tanh
 P = 128
 BANK = 512
 PACK = 4
+WORDS = K // 2
 ROWS = 256
 TG = 4
 GROUPS = T // TG
 PAIRS = H // ROWS
 STEPS = PAIRS * GROUPS * 2
+LAST = STEPS - 1
 R, Z, N = 0, 1, 2
-MX_BANKS = 4
-TR_BANKS = 2
-BACK_BANKS = 2
-W1_SLOTS = (-3, 0, -1, -2, 1, -2, 2)
-X3V = False
-X3B = 4
-WQ_SLOTS = (-6, -5, -4, -3, -2, -2, -2)
-WZN0 = 1
-X2B = 2
-V_LAST = 0
-WARM = (5, 1)
-E_LAG = 3
-Z_LAG = 3
-T_LAG = E_LAG + 1
-F_LAG = E_LAG + 2
-Q_STEPS = [s for s in range(STEPS - 2) if s % 2 == 0]
-X_SLOTS = (-3, -2, -2)
-HEAD_ENG = "svsvsvs"
-V_COPY_UNTIL = 1
+BIAS_ROWS = 3 * H // P
+BIAS_COLUMNS = 32
+
+SUM_LAG = 3
+TURN_LAG = SUM_LAG + 1
+END_LAG = SUM_LAG + 2
+R_LEAD = 2
+
+VECTOR_FIRST = 2
+GPSIMD_STEPS = range(0, STEPS - 3, 2)
+QUANT_FIRST = 10
+QUANT_EVERY = 4
+SINGLE_STORES = 4
 
 
 def tile_grucellmodel_pa_kernel(tc, input_seq, W_ih, b_ih, gh, out):
@@ -60,48 +56,46 @@ def tile_grucellmodel_pa_kernel(tc, input_seq, W_ih, b_ih, gh, out):
         ctx.enter_context(tc.manual_schedule())
 
         def mx_bank():
-            return psum.tile([P, BANK], F32, name="mx_bank", tag="mx", bufs=MX_BANKS)
+            return psum.tile([P, BANK], F32, name="mx_bank", tag="mx", bufs=4)
 
-        def plain_bank(tag="plain"):
+        def plain_bank(tag):
             return psum.tile([P, BANK], F32, name="plain_bank", tag=tag, bufs=2)
 
-        x_raw = {}
-        w_raw = {}
-        gh_raw = {}
-
-        def load_x(g, halves):
-            raw = keep.tile([P, len(halves), 2 * K], BF16, name="x_raw_%d_%d" % (g, halves[0]))
-            nc.sync.dma_start(out=raw[:], in_=x_blocks[g][:, halves[0] : halves[-1] + 1, :])
-            for i, h in enumerate(halves):
-                x_raw[g, h] = raw[:, i, :]
-
-        def load_w(pair, gates):
-            raw = keep.tile([P, len(gates), 2 * K], BF16, name="w_raw_%d_%d" % (pair, gates[0]))
-            nc.sync.dma_start(out=raw[:], in_=w_blocks[pair][:, gates[0] : gates[-1] + 1, :])
-            for i, gate in enumerate(gates):
-                w_raw[pair, gate] = raw[:, i, :]
-
-        def load_gh(pairs):
-            raw = keep.tile([P, 3, len(pairs) * ROWS], BF16, name="gh_raw_%d" % pairs[0])
-            nc.sync.dma_start(out=raw[:], in_=gh_gates[:, :, pairs[0] * ROWS : (pairs[-1] + 1) * ROWS])
-            for i, pair in enumerate(pairs):
-                gh_raw[pair] = raw[:, :, i * ROWS : (i + 1) * ROWS]
-
-        bias_rows = keep.tile([P, P], BF16, name="bias_rows")
-        nc.vector.memset(bias_rows[:], 0.0)
-        nc.scalar.dma_start(out=bias_rows[0 : 3 * H // P, :], in_=b_ih.rearrange("(c p) -> c p", p=P))
-
         zeros = keep.tile([P, BANK], BF16, name="zeros")
-        nc.vector.memset(zeros[:], 0.0)
-        unread = keep.tile([P, 1], F32, name="unread")
-        nc.scalar.activation(out=unread[:], in_=zeros[:, 0:1], func=SIGMOID)
+        nc.gpsimd.memset(zeros[:].bitcast(U32), 0)
 
         def warm_up(count):
             bank = mx_bank()
             for i in range(count):
                 nc.tensor.matmul(bank[:], lhsT=zeros[:, 0:P], rhs=zeros[:], start=True, stop=True)
 
-        warm_up(WARM[0])
+        bias_rows = keep.tile([P, P], BF16, name="bias_rows")
+        nc.gpsimd.memset(bias_rows[:].bitcast(U32), 0)
+        nc.scalar.dma_start(out=bias_rows[0:BIAS_ROWS, :], in_=b_ih.rearrange("(c p) -> c p", p=P))
+
+        unread = keep.tile([P, 1], F32, name="unread")
+        nc.scalar.activation(out=unread[:], in_=zeros[:, 0:1], func=SIGMOID)
+        warm_up(4)
+
+        raw = {}
+
+        def load_x(g, halves):
+            tile = keep.tile([P, len(halves), 2 * K], BF16, name="x_raw_%d_%d" % (g, halves[0]))
+            nc.sync.dma_start(out=tile[:], in_=x_blocks[g][:, halves[0] : halves[-1] + 1, :])
+            for i, half in enumerate(halves):
+                raw["x", 2 * g + half] = tile[:, i, :]
+
+        def load_w(pair, gates):
+            tile = keep.tile([P, len(gates), 2 * K], BF16, name="w_raw_%d_%d" % (pair, gates[0]))
+            nc.sync.dma_start(out=tile[:], in_=w_blocks[pair][:, gates[0] : gates[-1] + 1, :])
+            for i, gate in enumerate(gates):
+                raw["w", 3 * pair + gate] = tile[:, i, :]
+
+        def load_gh(pairs):
+            tile = keep.tile([P, 3, len(pairs) * ROWS], BF16, name="gh_raw_%d" % pairs[0])
+            nc.sync.dma_start(out=tile[:], in_=gh_gates[:, :, pairs[0] * ROWS : (pairs[-1] + 1) * ROWS])
+            for i, pair in enumerate(pairs):
+                raw["gh", pair] = tile[:, :, i * ROWS : (i + 1) * ROWS]
 
         load_x(0, [0])
         load_w(0, [R])
@@ -111,10 +105,11 @@ def tile_grucellmodel_pa_kernel(tc, input_seq, W_ih, b_ih, gh, out):
         load_x(1, [1])
         load_w(0, [N])
         load_w(0, [Z])
+        load_gh([1])
         load_x(2, [0, 1])
         load_x(3, [0, 1])
-        load_gh([1, 2, 3])
         load_w(1, [R, Z, N])
+        load_gh([2, 3])
         load_w(2, [R, Z, N])
         load_w(3, [R, Z, N])
 
@@ -123,312 +118,281 @@ def tile_grucellmodel_pa_kernel(tc, input_seq, W_ih, b_ih, gh, out):
         ident16 = keep.tile([P, P], BF16, name="ident16")
         make_identity(nc, ident16[:])
 
-        x_codes = [keep.tile([P, TG * B], U32, name="x_codes_%d" % g, align_bytes=64) for g in range(GROUPS)]
-        x_scales = [keep.tile([P, TG * B], U8, name="x_scales_%d" % g, align_bytes=64) for g in range(GROUPS)]
-        w_codes = [keep.tile([P, 3 * ROWS], U32, name="w_codes_%d" % q, align_bytes=64) for q in range(PAIRS)]
-        w_scales = [keep.tile([P, 3 * ROWS], U8, name="w_scales_%d" % q, align_bytes=64) for q in range(PAIRS)]
-        x_grouped = [keep.tile([P, TG * B * PACK], BF16, name="x_grouped_%d" % g, align_bytes=64) for g in range(GROUPS)]
-        w_grouped = [keep.tile([P, 3 * ROWS * PACK], BF16, name="w_grouped_%d" % q, align_bytes=64) for q in range(PAIRS)]
-        gh_t = [keep.tile([P, 4, B], F32, name="gh_t_%d" % q) for q in range(PAIRS)]
-        c_z = [keep.tile([P, ROWS], F32, name="c_z_%d" % q) for q in range(PAIRS)]
-        bias_t = keep.tile([P, 32], F32, name="bias_t")
-        turned = {}
+        columns = {"x": T * B, "w": 3 * H}
+        formats = {"x": X_FORMAT, "w": W_FORMAT}
+        codes = {m: keep.tile([P, c], U32, name=m + "_codes", align_bytes=64) for m, c in columns.items()}
+        scales = {m: keep.tile([P, c], U8, name=m + "_scales", align_bytes=64) for m, c in columns.items()}
+        grouped = {m: keep.tile([P, c * PACK], BF16, name=m + "_grouped", align_bytes=64) for m, c in columns.items()}
+        gh_t = [keep.tile([P, 4, B], F32, name="gh_t_%d" % pair) for pair in range(PAIRS)]
+        c_z = [keep.tile([P, ROWS], F32, name="c_z_%d" % pair) for pair in range(PAIRS)]
+        bias_t = keep.tile([P, BIAS_COLUMNS], F32, name="bias_t")
+        filled = {}
 
-        def copy_on(engine, dst, src):
-            if engine is nc.scalar:
-                nc.scalar.copy(out=dst, in_=src)
-            else:
-                nc.vector.tensor_copy(out=dst, in_=src)
-
-        def turn(key, raw, tag="plain"):
+        def fill(item, tag="operand"):
+            kind, index = item
             bank = plain_bank(tag)
-            words = raw.bitcast(F32)
-            for j in range(2):
-                for u in range(2):
-                    c = (2 * j + u) * P
-                    nc.tensor.transpose(bank[:, c : c + P], words[:, j * 256 + u : (j + 1) * 256 : 2], ident32[:])
-            turned[key] = bank
+            if kind == "gh":
+                for i, gate in enumerate((R, N)):
+                    for j in range(2):
+                        nc.tensor.matmul(
+                            bank[:, (2 * i + j) * P : (2 * i + j + 1) * P],
+                            lhsT=raw["gh", index][:, gate, j * P : (j + 1) * P], rhs=ident16[:], start=True, stop=True,
+                        )
+            elif kind == "cz":
+                nc.tensor.matmul(bank[:, 0:ROWS], lhsT=ident16[:], rhs=raw["gh", index][:, Z, :], start=True, stop=False)
+                for j in range(2):
+                    row = Z * (H // P) + 2 * index + j
+                    nc.tensor.matmul(
+                        bank[:, j * P : (j + 1) * P], lhsT=ident16[:, row : row + 1].to_broadcast([P, P]),
+                        rhs=bias_rows[:], start=False, stop=(j == 1),
+                    )
+            else:
+                words = raw[item].bitcast(F32)
+                for j in range(2):
+                    for u in range(2):
+                        nc.tensor.transpose(
+                            bank[:, (2 * j + u) * P : (2 * j + u + 1) * P],
+                            words[:, j * WORDS + u : (j + 1) * WORDS : 2], ident32[:],
+                        )
+            filled[item] = bank
 
-        def interleave(key, grouped, block, engine):
-            dst = grouped[:, block * ROWS * PACK : (block + 1) * ROWS * PACK].bitcast(F32)
-            copy_on(
-                engine,
-                dst.rearrange("q (p j u) -> q p j u", j=2, u=2),
-                turned[key][:].rearrange("q (j u p) -> q p j u", j=2, u=2),
-            )
+        def empty(item, copy):
+            kind, index = item
+            if kind == "gh":
+                copy(out=gh_t[index][:].rearrange("p i b -> p (i b)"), in_=filled[item][:])
+            elif kind == "cz":
+                copy(out=c_z[index][:], in_=filled[item][:, 0:ROWS])
+            else:
+                words = grouped[kind][:, index * ROWS * PACK : (index + 1) * ROWS * PACK].bitcast(F32)
+                copy(
+                    out=words.rearrange("q (p j u) -> q p j u", j=2, u=2),
+                    in_=filled[item][:].rearrange("q (j u p) -> q p j u", j=2, u=2),
+                )
 
-        def quantize(fmt, codes, scales, grouped, first, count):
+        def quantize(kind, first, count):
             cols = slice(first * ROWS, (first + count) * ROWS)
             nc.vector.quantize_mx(
-                out=codes[:, cols].bitcast(fmt),
-                scales=scales[:, cols],
-                in_=grouped[:, first * ROWS * PACK : (first + count) * ROWS * PACK],
+                out=codes[kind][:, cols].bitcast(formats[kind]), scales=scales[kind][:, cols],
+                in_=grouped[kind][:, cols.start * PACK : cols.stop * PACK],
             )
-
-        def turn_gh(pair, tag="plain"):
-            bank = plain_bank(tag)
-            for i, gate in enumerate((R, N)):
-                for j in range(2):
-                    c = (2 * i + j) * P
-                    nc.tensor.matmul(
-                        bank[:, c : c + P], lhsT=gh_raw[pair][:, gate, j * P : (j + 1) * P], rhs=ident16[:],
-                        start=True, stop=True,
-                    )
-            turned["gh", pair] = bank
-
-        def spread_z(pair):
-            bank = plain_bank()
-            nc.tensor.matmul(bank[:, 0:ROWS], lhsT=ident16[:], rhs=gh_raw[pair][:, Z, :], start=True, stop=False)
-            for j in range(2):
-                c = H // P + 2 * pair + j
-                nc.tensor.matmul(
-                    bank[:, j * P : (j + 1) * P], lhsT=ident16[:, c : c + 1].to_broadcast([P, P]), rhs=bias_rows[:],
-                    start=False, stop=(j == 1),
-                )
-            turned["cz", pair] = bank
 
         def turn_bias():
             bank = mx_bank()
-            nc.tensor.matmul(bank[:, 0:32], lhsT=bias_rows[:], rhs=ident16[:, 0:32], start=True, stop=True)
-            nc.vector.tensor_copy(out=bias_t[:], in_=bank[:, 0:32])
-
-        def keep_gh(pair, engine):
-            copy_on(engine, gh_t[pair][:].rearrange("p i b -> p (i b)"), turned["gh", pair][:])
-
-        def keep_cz(pair, engine):
-            copy_on(engine, c_z[pair][:], turned["cz", pair][:, 0:ROWS])
+            nc.tensor.matmul(
+                bank[:, 0:BIAS_COLUMNS], lhsT=bias_rows[:], rhs=ident16[:, 0:BIAS_COLUMNS], start=True, stop=True
+            )
+            nc.vector.tensor_copy(out=bias_t[:], in_=bank[:, 0:BIAS_COLUMNS])
 
         def place(s):
             return s // (2 * GROUPS), (s // 2) % GROUPS, s % 2
 
         sums = {}
-        vals = {}
+        tiles = {}
+
+        def matmul_mx(acc, stationary, moving):
+            (m0, cols0), (m1, cols1) = stationary, moving
+            nc.tensor.matmul_mx(
+                out=acc,
+                lhsT=codes[m0][:, cols0].bitcast(formats[m0]), lhsT_scale=scales[m0][:, cols0],
+                rhs=codes[m1][:, cols1].bitcast(formats[m1]), rhs_scale=scales[m1][:, cols1],
+                start=True, stop=True,
+            )
 
         def multiply(s, gate):
             pair, g, j = place(s)
             bank = mx_bank()
+            block = (3 * pair + gate) * ROWS
             if gate == Z:
-                w_cols = slice(Z * ROWS, (Z + 1) * ROWS)
                 for i in range(2):
-                    x_cols = slice((2 * j + i) * B, (2 * j + i + 1) * B)
-                    nc.tensor.matmul_mx(
-                        out=bank[:, i * ROWS : (i + 1) * ROWS],
-                        lhsT=x_codes[g][:, x_cols].bitcast(X_FORMAT), lhsT_scale=x_scales[g][:, x_cols],
-                        rhs=w_codes[pair][:, w_cols].bitcast(W_FORMAT), rhs_scale=w_scales[pair][:, w_cols],
-                        start=True, stop=True,
+                    token = (TG * g + 2 * j + i) * B
+                    matmul_mx(
+                        bank[:, i * ROWS : (i + 1) * ROWS],
+                        ("x", slice(token, token + B)), ("w", slice(block, block + ROWS)),
                     )
             else:
-                w_cols = slice(gate * ROWS + j * P, gate * ROWS + (j + 1) * P)
-                nc.tensor.matmul_mx(
-                    out=bank[:],
-                    lhsT=w_codes[pair][:, w_cols].bitcast(W_FORMAT), lhsT_scale=w_scales[pair][:, w_cols],
-                    rhs=x_codes[g][:].bitcast(X_FORMAT), rhs_scale=x_scales[g][:],
-                    start=True, stop=True,
+                matmul_mx(
+                    bank[:],
+                    ("w", slice(block + j * P, block + (j + 1) * P)), ("x", slice(g * TG * B, (g + 1) * TG * B)),
                 )
             sums[s, gate] = bank
 
         def by_t(ap):
-            return ap.rearrange("p (t b) -> p t b", b=P)
+            return ap.rearrange("p (t c) -> p t c", t=TG)
 
         def bias(s, gate):
             pair, g, j = place(s)
             c = gate * (H // P) + 2 * pair + j
             return bias_t[:, c : c + 1]
 
-        def add_r(s):
+        def gate_r(s):
             pair, g, j = place(s)
-            pre_r = work.tile([P, BANK], F32, name="pre_r", bufs=4)
+            pre_r = work.tile([P, BANK], F32, name="pre_r")
             nc.vector.tensor_tensor(
                 out=by_t(pre_r[:]), in0=by_t(sums[s, R][:]),
                 in1=gh_t[pair][:, j : j + 1, :].to_broadcast([P, TG, B]), op=ADD,
             )
-            vals["pre_r", s] = pre_r
+            tiles["r", s] = work.tile([P, BANK], F32, name="r")
+            nc.scalar.activation(out=tiles["r", s][:], in_=pre_r[:], func=SIGMOID, bias=bias(s, R))
 
-        def gate_r(s):
-            r = work.tile([P, BANK], F32, name="r", bufs=4)
-            nc.scalar.activation(out=r[:], in_=vals["pre_r", s][:], func=SIGMOID, bias=bias(s, R))
-            vals["r", s] = r
-
-        def scale_hn(s, engine):
+        def scale_gh_n(s, engine):
             pair, g, j = place(s)
-            rh = work.tile([P, BANK], F32, name="rh", bufs=5)
+            tiles["r_gh", s] = work.tile([P, BANK], F32, name="r_gh", bufs=SUM_LAG + 3)
             engine.tensor_tensor(
-                out=by_t(rh[:]), in0=by_t(vals["r", s][:]),
+                out=by_t(tiles["r_gh", s][:]), in0=by_t(tiles["r", s][:]),
                 in1=gh_t[pair][:, 2 + j : 3 + j, :].to_broadcast([P, TG, B]), op=MULT,
             )
-            vals["rh", s] = rh
-
-        def add_z(s):
-            pair, g, j = place(s)
-            pre_z = work.tile([P, 2, ROWS], F32, name="pre_z", bufs=4)
-            nc.vector.tensor_tensor(
-                out=pre_z[:], in0=sums[s, Z][:].rearrange("p (t c) -> p t c", t=2),
-                in1=c_z[pair][:].unsqueeze(1).to_broadcast([P, 2, ROWS]), op=ADD,
-            )
-            vals["pre_z", s] = pre_z
 
         def gate_z(s):
-            j = s % 2
-            if j == 0:
-                vals["keep_z", s // 2] = work.tile([P, TG, ROWS], F32, name="not_z", bufs=4)
-            nc.scalar.activation(
-                out=vals["keep_z", s // 2][:, 2 * j : 2 * j + 2, :], in_=vals["pre_z", s][:], func=SIGMOID, scale=-1.0
-            )
-
-        def add_n(s):
-            pre_n = work.tile([P, BANK], F32, name="pre_n", bufs=4)
-            if s in Q_STEPS:
-                nc.vector.scalar_tensor_tensor(
-                    out=pre_n[:], in0=sums[s, N][:], scalar=bias(s, N), in1=vals["rh", s][:], op0=ADD, op1=ADD
-                )
-            else:
-                nc.vector.tensor_tensor(out=pre_n[:], in0=sums[s, N][:], in1=vals["rh", s][:], op=ADD)
-            vals["pre_n", s] = pre_n
-
-        def tanh_first(s):
-            n = work.tile([P, BANK], F32, name="n_first", bufs=4)
-            nc.scalar.activation(out=n[:], in_=vals["pre_n", s][:], func=TANH, bias=bias(s, N))
-            vals["n", s] = n
-
-        def turn_back(s):
-            src = vals["pre_n", s] if s in Q_STEPS else vals["n", s]
-            bank = plain_bank("back")
-            for t in range(TG):
-                nc.tensor.transpose(bank[:, t * P : (t + 1) * P], src[:, t * B : (t + 1) * B], ident32[:])
-            vals["turned", s] = bank
-
-        def tanh_last(s):
-            n = work.tile([P, BANK], F32, name="n_last", bufs=4)
-            nc.scalar.activation(out=n[:], in_=vals["turned", s][:], func=TANH)
-            vals["n", s] = n
-
-        def finish(s):
             pair, g, j = place(s)
             if j == 0:
-                vals["h", s // 2] = work.tile([P, TG, ROWS], F32, name="h", bufs=4)
-            h = vals["h", s // 2][:, :, j * P : (j + 1) * P]
-            not_z = vals["keep_z", s // 2][:, :, j * P : (j + 1) * P]
-            if s in Q_STEPS:
-                nc.gpsimd.tensor_tensor(out=h, in0=by_t(vals["n", s][:]), in1=not_z, op=MULT)
+                tiles["pre_z", s // 2] = work.tile([P, TG, ROWS], F32, name="pre_z", bufs=2)
+                tiles["not_z", s // 2] = work.tile([P, TG, ROWS], F32, name="not_z")
+            pre_z = tiles["pre_z", s // 2][:, 2 * j : 2 * j + 2, :]
+            nc.vector.tensor_tensor(
+                out=pre_z, in0=sums[s, Z][:].rearrange("p (t c) -> p t c", t=2),
+                in1=c_z[pair][:].unsqueeze(1).to_broadcast([P, 2, ROWS]), op=ADD,
+            )
+            nc.scalar.activation(out=tiles["not_z", s // 2][:, 2 * j : 2 * j + 2, :], in_=pre_z, func=SIGMOID, scale=-1.0)
+
+        def sum_n(s, ts=range(TG)):
+            cols = slice(ts.start * B, ts.stop * B)
+            if ts.start == 0:
+                tiles["pre_n", s] = work.tile([P, BANK], F32, name="pre_n")
+            pre_n = tiles["pre_n", s][:, cols]
+            if s in GPSIMD_STEPS:
+                nc.vector.scalar_tensor_tensor(
+                    out=pre_n, in0=sums[s, N][:, cols], scalar=bias(s, N), in1=tiles["r_gh", s][:, cols],
+                    op0=ADD, op1=ADD,
+                )
             else:
-                nc.vector.tensor_tensor(out=h, in0=by_t(vals["turned", s][:]), in1=not_z, op=MULT)
-            rows = out[:, TG * g : TG * (g + 1), :]
-            if s >= STEPS - 2:
-                c = pair * ROWS + j * P
-                nc.sync.dma_start(out=rows[:, :, c : c + P], in_=h)
+                nc.vector.tensor_tensor(out=pre_n, in0=sums[s, N][:, cols], in1=tiles["r_gh", s][:, cols], op=ADD)
+                if ts.start == 0:
+                    tiles["n", s] = work.tile([P, BANK], F32, name="n_by_channel")
+                nc.scalar.activation(out=tiles["n", s][:, cols], in_=pre_n, func=TANH, bias=bias(s, N))
+
+        def turn_n(s, ts=range(TG), tag="turned"):
+            source = tiles["pre_n", s] if s in GPSIMD_STEPS else tiles["n", s]
+            bank = plain_bank(tag)
+            for t in ts:
+                nc.tensor.transpose(bank[:, t * P : (t + 1) * P], source[:, t * B : (t + 1) * B], ident32[:])
+            tiles["turned", s, ts.start] = bank
+
+        def tanh_turned(s):
+            tiles["n", s] = work.tile([P, BANK], F32, name="n_by_batch")
+            nc.scalar.activation(out=tiles["n", s][:], in_=tiles["turned", s, 0][:], func=TANH)
+
+        def finish(s, ts=range(TG)):
+            pair, g, j = place(s)
+            times = slice(ts.start, ts.stop)
+            if j == 0:
+                tiles["h", s // 2] = work.tile([P, TG, ROWS], F32, name="h")
+            h = tiles["h", s // 2][:, times, j * P : (j + 1) * P]
+            not_z = tiles["not_z", s // 2][:, times, j * P : (j + 1) * P]
+            if s in GPSIMD_STEPS:
+                nc.gpsimd.tensor_tensor(out=h, in0=by_t(tiles["n", s][:]), in1=not_z, op=MULT)
+            else:
+                nc.vector.tensor_tensor(
+                    out=h, in0=by_t(tiles["turned", s, ts.start][:])[:, times, :], in1=not_z, op=MULT
+                )
+            out_group = out[:, TG * g : TG * (g + 1), :]
+            if s >= STEPS - SINGLE_STORES:
+                channel = pair * ROWS + j * P
+                nc.sync.dma_start(out=out_group[:, times, channel : channel + P], in_=h)
             elif j == 1:
-                nc.sync.dma_start(out=rows[:, :, pair * ROWS : (pair + 1) * ROWS], in_=vals["h", s // 2][:])
+                nc.sync.dma_start(out=out_group[:, :, pair * ROWS : (pair + 1) * ROWS], in_=tiles["h", s // 2][:])
 
-        turn(("x", 0, 0), x_raw[0, 0])
-        turn(("w", 0, R), w_raw[0, R])
-        turn(("x", 0, 1), x_raw[0, 1], "back")
-        warm_up(WARM[1])
-        turn_gh(0, "back")
-        interleave(("x", 0, 0), x_grouped[0], 0, nc.scalar)
-        interleave(("w", 0, R), w_grouped[0], R, nc.vector)
-        interleave(("x", 0, 1), x_grouped[0], 1, nc.scalar)
-        quantize(X_FORMAT, x_codes[0], x_scales[0], x_grouped[0], 0, 1)
-        quantize(W_FORMAT, w_codes[0], w_scales[0], w_grouped[0], R, 1)
-        quantize(X_FORMAT, x_codes[0], x_scales[0], x_grouped[0], 1, 1)
-        keep_gh(0, nc.scalar)
+        on_scalar = nc.scalar.copy
+        on_vector = nc.vector.tensor_copy
+
+        fill(("x", 0))
+        fill(("w", R))
+        fill(("x", 1), "turned")
+        warm_up(2)
+        fill(("gh", 0), "turned")
+        empty(("x", 0), on_scalar)
+        empty(("w", R), on_vector)
+        empty(("x", 1), on_scalar)
+        quantize("x", 0, 1)
+        quantize("w", R, 1)
+        quantize("x", 1, 1)
+        empty(("gh", 0), on_scalar)
         turn_bias()
-        turn(("x", 1, 0), x_raw[1, 0])
-        multiply(0, R)
-        multiply(1, R)
-        turn(("x", 1, 1), x_raw[1, 1])
-        interleave(("x", 1, 0), x_grouped[1], 0, nc.vector)
-        interleave(("x", 1, 1), x_grouped[1], 1, nc.scalar)
-        turn(("w", 0, N), w_raw[0, N], "back")
-        turn(("w", 0, Z), w_raw[0, Z], "back")
+        fill(("x", 2))
+        fill(("x", 3))
+        for s in range(R_LEAD):
+            multiply(s, R)
+        empty(("x", 2), on_vector)
+        empty(("x", 3), on_scalar)
+        fill(("w", N), "turned")
+        fill(("w", Z), "turned")
 
-        turns = {}
-        copies = {}
-        v_copies = {}
-        quants = {}
-        early_quants = {}
-
-        def ride(slot, turn_job, copy_job, on_vector=False):
-            turns.setdefault(slot - 1, []).append(turn_job)
-            if on_vector:
-                v_copies.setdefault(slot, []).append(lambda: copy_job(nc.vector))
-            else:
-                copies.setdefault(slot, []).append(lambda: copy_job(nc.scalar))
-
-        def ride_x(slot, g, h, v=False):
-            ride(slot, lambda: turn(("x", g, h), x_raw[g, h]), lambda e: interleave(("x", g, h), x_grouped[g], h, e), v)
-
-        def ride_w(slot, q, gate, v=False):
-            ride(slot, lambda: turn(("w", q, gate), w_raw[q, gate]), lambda e: interleave(("w", q, gate), w_grouped[q], gate, e), v)
-
-        def quant_x(slot, g, table=early_quants):
-            table.setdefault(slot, []).append(lambda: quantize(X_FORMAT, x_codes[g], x_scales[g], x_grouped[g], 0, 2))
-
-        def quant_w(slot, q, first, count, table=early_quants):
-            table.setdefault(slot, []).append(lambda: quantize(W_FORMAT, w_codes[q], w_scales[q], w_grouped[q], first, count))
-
-        quant_x(0, 1, quants)
-        v_copies[0] = [lambda: interleave(("w", 0, N), w_grouped[0], N, nc.vector)]
-        copies[1] = [lambda: interleave(("w", 0, Z), w_grouped[0], Z, nc.scalar)]
-        quant_w(WZN0, 0, Z, 2, quants)
-        ride(1, lambda: spread_z(0), lambda e: keep_cz(0, e), True)
-        ride_x(1, 2, 0)
-        ride_x(2, 2, 1)
-        quant_x(2, 2, quants)
-        ride_x(3, 3, 0, X3V)
-        ride_x(X3B, 3, 1)
-        quant_x(4, 3, early_quants if X3B == 3 else quants)
-        for q in range(1, PAIRS):
-            first = 8 * q
-            slots = W1_SLOTS if q == 1 else WQ_SLOTS
-            ride_w(first + slots[0], q, R)
-            ride_w(first + slots[1], q, Z)
-            ride_w(first + slots[2], q, N)
-            ride(first + slots[3], lambda q=q: turn_gh(q), lambda e, q=q: keep_gh(q, e))
-            ride(first + slots[4], lambda q=q: spread_z(q), lambda e, q=q: keep_cz(q, e))
-            if q == 1:
-                quant_w(first + slots[5], q, R, 1)
-                quant_w(first + slots[6], q, Z, 2)
-            else:
-                quant_w(first + slots[5], q, R, 2)
-                quant_w(first + slots[6], q, N, 1)
+        rides = {1 + i: ("x", 4 + i) for i in range(4)}
+        rides[5] = ("w", 3)
+        behind_add = {0: ("x", 2, 2), QUANT_FIRST - QUANT_EVERY: ("w", 3, 1)}
+        at_end = {1: ("w", Z, 2), 2: ("x", 4, 2), 4: ("x", 6, 2)}
+        for i, first in enumerate(range(4, 3 * PAIRS, 2)):
+            slot = QUANT_FIRST + QUANT_EVERY * i
+            behind_add[slot] = ("w", first, 2)
+            rides[slot - 3] = ("w", first)
+            rides[slot - 1] = ("w", first + 1)
+        for i in range(2 * (PAIRS - 1)):
+            rides[QUANT_FIRST + QUANT_EVERY * (i - 1)] = ("gh" if i % 2 == 0 else "cz", 1 + i // 2)
 
         def live(s):
             return 0 <= s < STEPS
 
-        for slot in range(STEPS + F_LAG):
-            for job in copies.get(slot, []):
-                job()
+        def multiply_n_and_z(s):
+            multiply(s, N)
+            multiply(s, Z)
+
+        for slot in range(LAST + SUM_LAG):
+            if slot == 1:
+                empty(("w", Z), on_scalar)
+            if slot in rides:
+                empty(rides[slot], on_scalar)
             if live(slot):
-                add_r(slot)
                 gate_r(slot)
-                if slot < STEPS - V_LAST:
-                    scale_hn(slot, nc.gpsimd)
-            for job in early_quants.get(slot, []):
-                job()
-            for job in v_copies.get(slot, []):
-                job()
-            if live(slot - T_LAG):
-                turn_back(slot - T_LAG)
-            for job in turns.get(slot, []):
-                job()
-            if live(slot - 1) and slot - 1 >= STEPS - V_LAST:
-                scale_hn(slot - 1, nc.vector)
-            if live(slot - E_LAG):
-                add_n(slot - E_LAG)
-                if slot - E_LAG not in Q_STEPS:
-                    tanh_first(slot - E_LAG)
-            if live(slot - T_LAG) and slot - T_LAG in Q_STEPS:
-                tanh_last(slot - T_LAG)
-            if live(slot - Z_LAG):
-                add_z(slot - Z_LAG)
-                gate_z(slot - Z_LAG)
-            if live(slot - F_LAG):
-                finish(slot - F_LAG)
-            for job in quants.get(slot, []):
-                job()
-            if live(slot - E_LAG + 1):
-                multiply(slot - E_LAG + 1, N)
-            if live(slot - Z_LAG + 1):
-                multiply(slot - Z_LAG + 1, Z)
-            if live(slot + 2):
-                multiply(slot + 2, R)
+                if slot >= VECTOR_FIRST:
+                    scale_gh_n(slot, nc.gpsimd)
+            if slot in behind_add:
+                quantize(*behind_add[slot])
+            if slot == 0:
+                empty(("w", N), on_scalar)
+            if slot == 1:
+                empty(("cz", 0), on_vector)
+            if slot >= STEPS:
+                multiply_n_and_z(slot + 1 - SUM_LAG)
+            if live(slot - TURN_LAG):
+                turn_n(slot - TURN_LAG)
+            if slot == 0:
+                fill(("cz", 0))
+            if slot + 1 in rides:
+                fill(rides[slot + 1])
+            if 0 <= slot - 1 < VECTOR_FIRST:
+                scale_gh_n(slot - 1, nc.vector)
+            if live(slot - SUM_LAG):
+                sum_n(slot - SUM_LAG)
+            if slot - TURN_LAG in GPSIMD_STEPS:
+                tanh_turned(slot - TURN_LAG)
+            if live(slot - SUM_LAG):
+                gate_z(slot - SUM_LAG)
+            if live(slot - END_LAG):
+                finish(slot - END_LAG)
+            if slot in at_end:
+                quantize(*at_end[slot])
+            if slot < STEPS and live(slot + 1 - SUM_LAG):
+                multiply_n_and_z(slot + 1 - SUM_LAG)
+            if live(slot + R_LEAD):
+                multiply(slot + R_LEAD, R)
+
+        halves = (range(0, 2), range(2, TG))
+        turn_n(LAST - 1)
+        gate_z(LAST)
+        for ts in halves:
+            sum_n(LAST, ts)
+        finish(LAST - 2)
+        for ts, tag in zip(halves, ("turned", "operand")):
+            turn_n(LAST, ts, tag)
+        finish(LAST - 1)
+        for ts in halves:
+            finish(LAST, ts)

from contextlib import ExitStack

import concourse.mybir as mybir
from concourse.masks import make_identity

T, B, K, H = 16, 128, 512, 1024
FLOPS = 2 * T * B * K * 3 * H

F32 = mybir.dt.float32
BF16 = mybir.dt.bfloat16
U32 = mybir.dt.uint32
U8 = mybir.dt.uint8
X_FORMAT = mybir.dt.float8_e5m2_x4
W_FORMAT = mybir.dt.float8_e4m3fn_x4
ADD = mybir.AluOpType.add
MULT = mybir.AluOpType.mult
SIGMOID = mybir.ActivationFunctionType.Sigmoid
TANH = mybir.ActivationFunctionType.Tanh

P = 128
BANK = 512
PACK = 4
WORDS = K // 2
ROWS = 256
TG = 4
GROUPS = T // TG
PAIRS = H // ROWS
STEPS = PAIRS * GROUPS * 2
LAST = STEPS - 1
R, Z, N = 0, 1, 2
BIAS_ROWS = 3 * H // P
BIAS_COLUMNS = 32

SUM_LAG = 3
TURN_LAG = SUM_LAG + 1
END_LAG = SUM_LAG + 2
R_LEAD = 2

VECTOR_FIRST = 2
GPSIMD_STEPS = range(0, STEPS - 3, 2)
QUANT_FIRST = 10
QUANT_EVERY = 4
SINGLE_STORES = 4


def tile_grucellmodel_pa_kernel(tc, input_seq, W_ih, b_ih, gh, out):
    nc = tc.nc
    x_blocks = input_seq.rearrange("t b k -> (t b) k").rearrange("(g h p j) k -> g p h (j k)", h=2, p=P, j=2)
    w_blocks = W_ih.rearrange("(gate pair p j) k -> pair p gate (j k)", gate=3, p=P, j=2)
    gh_gates = gh.rearrange("b (gate c) -> b gate c", gate=3)

    with ExitStack() as ctx:
        keep = ctx.enter_context(tc.tile_pool(name="keep", bufs=1))
        work = ctx.enter_context(tc.tile_pool(name="work", bufs=4))
        psum = ctx.enter_context(tc.psum_pool(name="psum", bufs=1))
        ctx.enter_context(tc.manual_schedule())

        def mx_bank():
            return psum.tile([P, BANK], F32, name="mx_bank", tag="mx", bufs=4)

        def plain_bank(tag):
            return psum.tile([P, BANK], F32, name="plain_bank", tag=tag, bufs=2)

        zeros = keep.tile([P, BANK], BF16, name="zeros")
        nc.gpsimd.memset(zeros[:].bitcast(U32), 0)

        def warm_up(count):
            bank = mx_bank()
            for i in range(count):
                nc.tensor.matmul(bank[:], lhsT=zeros[:, 0:P], rhs=zeros[:], start=True, stop=True)

        bias_rows = keep.tile([P, P], BF16, name="bias_rows")
        nc.gpsimd.memset(bias_rows[:].bitcast(U32), 0)
        nc.scalar.dma_start(out=bias_rows[0:BIAS_ROWS, :], in_=b_ih.rearrange("(c p) -> c p", p=P))

        unread = keep.tile([P, 1], F32, name="unread")
        nc.scalar.activation(out=unread[:], in_=zeros[:, 0:1], func=SIGMOID)
        warm_up(4)

        raw = {}

        def load_x(g, halves):
            tile = keep.tile([P, len(halves), 2 * K], BF16, name="x_raw_%d_%d" % (g, halves[0]))
            nc.sync.dma_start(out=tile[:], in_=x_blocks[g][:, halves[0] : halves[-1] + 1, :])
            for i, half in enumerate(halves):
                raw["x", 2 * g + half] = tile[:, i, :]

        def load_w(pair, gates):
            tile = keep.tile([P, len(gates), 2 * K], BF16, name="w_raw_%d_%d" % (pair, gates[0]))
            nc.sync.dma_start(out=tile[:], in_=w_blocks[pair][:, gates[0] : gates[-1] + 1, :])
            for i, gate in enumerate(gates):
                raw["w", 3 * pair + gate] = tile[:, i, :]

        def load_gh(pairs):
            tile = keep.tile([P, 3, len(pairs) * ROWS], BF16, name="gh_raw_%d" % pairs[0])
            nc.sync.dma_start(out=tile[:], in_=gh_gates[:, :, pairs[0] * ROWS : (pairs[-1] + 1) * ROWS])
            for i, pair in enumerate(pairs):
                raw["gh", pair] = tile[:, :, i * ROWS : (i + 1) * ROWS]

        load_x(0, [0])
        load_w(0, [R])
        load_x(0, [1])
        load_gh([0])
        load_x(1, [0])
        load_x(1, [1])
        load_w(0, [N])
        load_w(0, [Z])
        load_gh([1])
        load_x(2, [0, 1])
        load_x(3, [0, 1])
        load_w(1, [R, Z, N])
        load_gh([2, 3])
        load_w(2, [R, Z, N])
        load_w(3, [R, Z, N])

        ident32 = keep.tile([P, P], F32, name="ident32")
        make_identity(nc, ident32[:])
        ident16 = keep.tile([P, P], BF16, name="ident16")
        make_identity(nc, ident16[:])

        columns = {"x": T * B, "w": 3 * H}
        formats = {"x": X_FORMAT, "w": W_FORMAT}
        codes = {m: keep.tile([P, c], U32, name=m + "_codes", align_bytes=64) for m, c in columns.items()}
        scales = {m: keep.tile([P, c], U8, name=m + "_scales", align_bytes=64) for m, c in columns.items()}
        grouped = {m: keep.tile([P, c * PACK], BF16, name=m + "_grouped", align_bytes=64) for m, c in columns.items()}
        gh_t = [keep.tile([P, 4, B], F32, name="gh_t_%d" % pair) for pair in range(PAIRS)]
        c_z = [keep.tile([P, ROWS], F32, name="c_z_%d" % pair) for pair in range(PAIRS)]
        bias_t = keep.tile([P, BIAS_COLUMNS], F32, name="bias_t")
        filled = {}

        def fill(item, tag="operand"):
            kind, index = item
            bank = plain_bank(tag)
            if kind == "gh":
                for i, gate in enumerate((R, N)):
                    for j in range(2):
                        nc.tensor.matmul(
                            bank[:, (2 * i + j) * P : (2 * i + j + 1) * P],
                            lhsT=raw["gh", index][:, gate, j * P : (j + 1) * P], rhs=ident16[:], start=True, stop=True,
                        )
            elif kind == "cz":
                nc.tensor.matmul(bank[:, 0:ROWS], lhsT=ident16[:], rhs=raw["gh", index][:, Z, :], start=True, stop=False)
                for j in range(2):
                    row = Z * (H // P) + 2 * index + j
                    nc.tensor.matmul(
                        bank[:, j * P : (j + 1) * P], lhsT=ident16[:, row : row + 1].to_broadcast([P, P]),
                        rhs=bias_rows[:], start=False, stop=(j == 1),
                    )
            else:
                words = raw[item].bitcast(F32)
                for j in range(2):
                    for u in range(2):
                        nc.tensor.transpose(
                            bank[:, (2 * j + u) * P : (2 * j + u + 1) * P],
                            words[:, j * WORDS + u : (j + 1) * WORDS : 2], ident32[:],
                        )
            filled[item] = bank

        def empty(item, copy):
            kind, index = item
            if kind == "gh":
                copy(out=gh_t[index][:].rearrange("p i b -> p (i b)"), in_=filled[item][:])
            elif kind == "cz":
                copy(out=c_z[index][:], in_=filled[item][:, 0:ROWS])
            else:
                words = grouped[kind][:, index * ROWS * PACK : (index + 1) * ROWS * PACK].bitcast(F32)
                copy(
                    out=words.rearrange("q (p j u) -> q p j u", j=2, u=2),
                    in_=filled[item][:].rearrange("q (j u p) -> q p j u", j=2, u=2),
                )

        def quantize(kind, first, count):
            cols = slice(first * ROWS, (first + count) * ROWS)
            nc.vector.quantize_mx(
                out=codes[kind][:, cols].bitcast(formats[kind]), scales=scales[kind][:, cols],
                in_=grouped[kind][:, cols.start * PACK : cols.stop * PACK],
            )

        def turn_bias():
            bank = mx_bank()
            nc.tensor.matmul(
                bank[:, 0:BIAS_COLUMNS], lhsT=bias_rows[:], rhs=ident16[:, 0:BIAS_COLUMNS], start=True, stop=True
            )
            nc.vector.tensor_copy(out=bias_t[:], in_=bank[:, 0:BIAS_COLUMNS])

        def place(s):
            return s // (2 * GROUPS), (s // 2) % GROUPS, s % 2

        sums = {}
        tiles = {}

        def matmul_mx(acc, stationary, moving):
            (m0, cols0), (m1, cols1) = stationary, moving
            nc.tensor.matmul_mx(
                out=acc,
                lhsT=codes[m0][:, cols0].bitcast(formats[m0]), lhsT_scale=scales[m0][:, cols0],
                rhs=codes[m1][:, cols1].bitcast(formats[m1]), rhs_scale=scales[m1][:, cols1],
                start=True, stop=True,
            )

        def multiply(s, gate):
            pair, g, j = place(s)
            bank = mx_bank()
            block = (3 * pair + gate) * ROWS
            if gate == Z:
                for i in range(2):
                    token = (TG * g + 2 * j + i) * B
                    matmul_mx(
                        bank[:, i * ROWS : (i + 1) * ROWS],
                        ("x", slice(token, token + B)), ("w", slice(block, block + ROWS)),
                    )
            else:
                matmul_mx(
                    bank[:],
                    ("w", slice(block + j * P, block + (j + 1) * P)), ("x", slice(g * TG * B, (g + 1) * TG * B)),
                )
            sums[s, gate] = bank

        def by_t(ap):
            return ap.rearrange("p (t c) -> p t c", t=TG)

        def bias(s, gate):
            pair, g, j = place(s)
            c = gate * (H // P) + 2 * pair + j
            return bias_t[:, c : c + 1]

        def gate_r(s):
            pair, g, j = place(s)
            pre_r = work.tile([P, BANK], F32, name="pre_r")
            nc.vector.tensor_tensor(
                out=by_t(pre_r[:]), in0=by_t(sums[s, R][:]),
                in1=gh_t[pair][:, j : j + 1, :].to_broadcast([P, TG, B]), op=ADD,
            )
            tiles["r", s] = work.tile([P, BANK], F32, name="r")
            nc.scalar.activation(out=tiles["r", s][:], in_=pre_r[:], func=SIGMOID, bias=bias(s, R))

        def scale_gh_n(s, engine):
            pair, g, j = place(s)
            tiles["r_gh", s] = work.tile([P, BANK], F32, name="r_gh", bufs=SUM_LAG + 3)
            engine.tensor_tensor(
                out=by_t(tiles["r_gh", s][:]), in0=by_t(tiles["r", s][:]),
                in1=gh_t[pair][:, 2 + j : 3 + j, :].to_broadcast([P, TG, B]), op=MULT,
            )

        def gate_z(s):
            pair, g, j = place(s)
            if j == 0:
                tiles["pre_z", s // 2] = work.tile([P, TG, ROWS], F32, name="pre_z", bufs=2)
                tiles["not_z", s // 2] = work.tile([P, TG, ROWS], F32, name="not_z")
            pre_z = tiles["pre_z", s // 2][:, 2 * j : 2 * j + 2, :]
            nc.vector.tensor_tensor(
                out=pre_z, in0=sums[s, Z][:].rearrange("p (t c) -> p t c", t=2),
                in1=c_z[pair][:].unsqueeze(1).to_broadcast([P, 2, ROWS]), op=ADD,
            )
            nc.scalar.activation(out=tiles["not_z", s // 2][:, 2 * j : 2 * j + 2, :], in_=pre_z, func=SIGMOID, scale=-1.0)

        def sum_n(s, ts=range(TG)):
            cols = slice(ts.start * B, ts.stop * B)
            if ts.start == 0:
                tiles["pre_n", s] = work.tile([P, BANK], F32, name="pre_n")
            pre_n = tiles["pre_n", s][:, cols]
            if s in GPSIMD_STEPS:
                nc.vector.scalar_tensor_tensor(
                    out=pre_n, in0=sums[s, N][:, cols], scalar=bias(s, N), in1=tiles["r_gh", s][:, cols],
                    op0=ADD, op1=ADD,
                )
            else:
                nc.vector.tensor_tensor(out=pre_n, in0=sums[s, N][:, cols], in1=tiles["r_gh", s][:, cols], op=ADD)
                if ts.start == 0:
                    tiles["n", s] = work.tile([P, BANK], F32, name="n_by_channel")
                nc.scalar.activation(out=tiles["n", s][:, cols], in_=pre_n, func=TANH, bias=bias(s, N))

        def turn_n(s, ts=range(TG), tag="turned"):
            source = tiles["pre_n", s] if s in GPSIMD_STEPS else tiles["n", s]
            bank = plain_bank(tag)
            for t in ts:
                nc.tensor.transpose(bank[:, t * P : (t + 1) * P], source[:, t * B : (t + 1) * B], ident32[:])
            tiles["turned", s, ts.start] = bank

        def tanh_turned(s):
            tiles["n", s] = work.tile([P, BANK], F32, name="n_by_batch")
            nc.scalar.activation(out=tiles["n", s][:], in_=tiles["turned", s, 0][:], func=TANH)

        def finish(s, ts=range(TG)):
            pair, g, j = place(s)
            times = slice(ts.start, ts.stop)
            if j == 0:
                tiles["h", s // 2] = work.tile([P, TG, ROWS], F32, name="h")
            h = tiles["h", s // 2][:, times, j * P : (j + 1) * P]
            not_z = tiles["not_z", s // 2][:, times, j * P : (j + 1) * P]
            if s in GPSIMD_STEPS:
                nc.gpsimd.tensor_tensor(out=h, in0=by_t(tiles["n", s][:]), in1=not_z, op=MULT)
            else:
                nc.vector.tensor_tensor(
                    out=h, in0=by_t(tiles["turned", s, ts.start][:])[:, times, :], in1=not_z, op=MULT
                )
            out_group = out[:, TG * g : TG * (g + 1), :]
            if s >= STEPS - SINGLE_STORES:
                channel = pair * ROWS + j * P
                nc.sync.dma_start(out=out_group[:, times, channel : channel + P], in_=h)
            elif j == 1:
                nc.sync.dma_start(out=out_group[:, :, pair * ROWS : (pair + 1) * ROWS], in_=tiles["h", s // 2][:])

        on_scalar = nc.scalar.copy
        on_vector = nc.vector.tensor_copy

        fill(("x", 0))
        fill(("w", R))
        fill(("x", 1), "turned")
        warm_up(2)
        fill(("gh", 0), "turned")
        empty(("x", 0), on_scalar)
        empty(("w", R), on_vector)
        empty(("x", 1), on_scalar)
        quantize("x", 0, 1)
        quantize("w", R, 1)
        quantize("x", 1, 1)
        empty(("gh", 0), on_scalar)
        turn_bias()
        fill(("x", 2))
        fill(("x", 3))
        for s in range(R_LEAD):
            multiply(s, R)
        empty(("x", 2), on_vector)
        empty(("x", 3), on_scalar)
        fill(("w", N), "turned")
        fill(("w", Z), "turned")

        rides = {1 + i: ("x", 4 + i) for i in range(4)}
        rides[5] = ("w", 3)
        behind_add = {0: ("x", 2, 2), QUANT_FIRST - QUANT_EVERY: ("w", 3, 1)}
        at_end = {1: ("w", Z, 2), 2: ("x", 4, 2), 4: ("x", 6, 2)}
        for i, first in enumerate(range(4, 3 * PAIRS, 2)):
            slot = QUANT_FIRST + QUANT_EVERY * i
            behind_add[slot] = ("w", first, 2)
            rides[slot - 3] = ("w", first)
            rides[slot - 1] = ("w", first + 1)
        for i in range(2 * (PAIRS - 1)):
            rides[QUANT_FIRST + QUANT_EVERY * (i - 1)] = ("gh" if i % 2 == 0 else "cz", 1 + i // 2)

        def live(s):
            return 0 <= s < STEPS

        def multiply_n_and_z(s):
            multiply(s, N)
            multiply(s, Z)

        for slot in range(LAST + SUM_LAG):
            if slot == 1:
                empty(("w", Z), on_scalar)
            if slot in rides:
                empty(rides[slot], on_scalar)
            if live(slot):
                gate_r(slot)
                if slot >= VECTOR_FIRST:
                    scale_gh_n(slot, nc.gpsimd)
            if slot in behind_add:
                quantize(*behind_add[slot])
            if slot == 0:
                empty(("w", N), on_scalar)
            if slot == 1:
                empty(("cz", 0), on_vector)
            if slot >= STEPS:
                multiply_n_and_z(slot + 1 - SUM_LAG)
            if live(slot - TURN_LAG):
                turn_n(slot - TURN_LAG)
            if slot == 0:
                fill(("cz", 0))
            if slot + 1 in rides:
                fill(rides[slot + 1])
            if 0 <= slot - 1 < VECTOR_FIRST:
                scale_gh_n(slot - 1, nc.vector)
            if live(slot - SUM_LAG):
                sum_n(slot - SUM_LAG)
            if slot - TURN_LAG in GPSIMD_STEPS:
                tanh_turned(slot - TURN_LAG)
            if live(slot - SUM_LAG):
                gate_z(slot - SUM_LAG)
            if live(slot - END_LAG):
                finish(slot - END_LAG)
            if slot in at_end:
                quantize(*at_end[slot])
            if slot < STEPS and live(slot + 1 - SUM_LAG):
                multiply_n_and_z(slot + 1 - SUM_LAG)
            if live(slot + R_LEAD):
                multiply(slot + R_LEAD, R)

        halves = (range(0, 2), range(2, TG))
        turn_n(LAST - 1)
        gate_z(LAST)
        for ts in halves:
            sum_n(LAST, ts)
        finish(LAST - 2)
        for ts, tag in zip(halves, ("turned", "operand")):
            turn_n(LAST, ts, tag)
        finish(LAST - 1)
        for ts in halves:
            finish(LAST, ts)
